import numpy as np
import ml_dtypes


def mxq(x, axis, fmt="e4m3"):
    dtype, down = {"e4m3": (ml_dtypes.float8_e4m3fn, 7), "e5m2": (ml_dtypes.float8_e5m2, 14)}[fmt]
    v = np.moveaxis(np.asarray(x, np.float32).astype(ml_dtypes.bfloat16).astype(np.float64), axis, -1)
    blocks = v.reshape(v.shape[:-1] + (-1, 32))
    amax = np.abs(blocks).max(-1, keepdims=True)
    byte = np.maximum(np.where(amax > 0, np.frexp(amax)[1] - 1 + 127, 0) - down, 1)
    scale = np.exp2(byte - 127.0)
    codes = (blocks / scale).astype(np.float32).astype(dtype).astype(np.float64)
    return np.moveaxis((codes * scale).reshape(v.shape), -1, axis)


WIDE = False


def mx_kscale(k):
    if not WIDE:
        return np.ones(k)
    levels = np.array([30, -30])
    if k % 512:
        return np.exp2(np.random.permutation(np.resize(levels, k // 32))).repeat(32)
    a = np.empty((k // 512, 16))
    for p in range(k // 512):
        a[p, :8] = np.random.permutation(np.resize(levels, 8))
        for g in range(8):
            far = levels[np.abs(levels - a[p, g]) >= 10]
            a[p, g + 8] = far[np.random.randint(len(far))]
    return np.exp2(a.ravel()).repeat(32)


BF16 = ml_dtypes.bfloat16


def bf(x):
    return np.asarray(x, np.float32).astype(BF16)


def f64(x):
    return np.asarray(x).astype(np.float64)


E2M1 = np.array([0.0, 0.5, 1.0, 1.5, 2.0, 3.0, 4.0, 6.0, -0.0, -0.5, -1.0, -1.5, -2.0, -3.0, -4.0, -6.0])


def pack_weight(w, fmt):
    k, n = w.shape
    w = f64(bf(w)).reshape(k // 32, 32, n)
    amax = np.abs(w).max(1)
    if fmt == "e4m3":
        byte = np.frexp(amax)[1] - 1 + 127 - 7
    else:
        mant, ex = np.frexp(amax / 6.0)
        byte = np.where(mant > 0.5, ex, ex - 1) + 127
    byte = np.clip(np.where(amax > 0, byte, 1), 1, 254)
    scaled = (w * np.exp2(127.0 - byte)[:, None, :]).reshape(k, n).astype(np.float32)
    by_word = np.ascontiguousarray(scaled.reshape(k // 512, 128, 4, n).transpose(0, 1, 3, 2))
    if fmt == "e4m3":
        words = by_word.astype(ml_dtypes.float8_e4m3fn).view(np.uint8)
    else:
        c = by_word.astype(ml_dtypes.float4_e2m1fn).view(np.uint8) & 0xF
        words = c[..., 0::2] | (c[..., 1::2] << 4)
    return np.ascontiguousarray(words), np.ascontiguousarray(byte.astype(np.uint8).reshape(k // 512, 16, n))


def unpack_weight(words, scales, fmt):
    g, p, n, _ = words.shape
    if fmt == "e4m3":
        vals = np.ascontiguousarray(words).view(ml_dtypes.float8_e4m3fn).astype(np.float64)
    else:
        nib = np.empty((g, p, n, 4), np.uint8)
        nib[..., 0::2] = words & 0xF
        nib[..., 1::2] = words >> 4
        vals = E2M1[nib]
    vals = vals * np.repeat(np.exp2(scales.astype(np.float64) - 127.0), 8, axis=1)[..., None]
    return vals.transpose(0, 1, 3, 2).reshape(g * 512, n)

def pack4(w):
    words, scales = pack_weight(w, "e2m1")
    return words.reshape(words.shape[0], 128, -1), scales


def unpack4(words, scales):
    return unpack_weight(words.reshape(words.shape[0], 128, -1, 2), scales, "e2m1")


B, IN, H = 512, 1024, 1024


def sigmoid(v):
    return 1.0 / (1.0 + np.exp(-v))


def setup_inputs():
    s, t = mx_kscale(IN), mx_kscale(H)
    a = np.sqrt(2.0 / (IN + H))
    x = bf(np.random.standard_normal((B, IN)) * s)
    h_prev = bf(np.random.standard_normal((B, H)) * t)
    m_prev = bf(np.random.standard_normal((B, H)) * 0.5)
    Wi_x_words, Wi_x_scales = pack4((np.random.standard_normal((H, IN)) * a / s).T)
    b_i = bf(np.random.standard_normal(H) * 0.3)
    Wi_h_words, Wi_h_scales = pack4((np.random.standard_normal((H, H)) * a / t).T)
    Wf_x_words, Wf_x_scales = pack4((np.random.standard_normal((H, IN)) * a / s).T)
    b_f = bf(2.0 + np.random.standard_normal(H) * 0.3)
    Wf_h_words, Wf_h_scales = pack4((np.random.standard_normal((H, H)) * a / t).T)
    return {
        "x": x,
        "h_prev": h_prev,
        "m_prev": m_prev,
        "Wi_x_words": Wi_x_words,
        "Wi_x_scales": Wi_x_scales,
        "b_i": b_i,
        "Wi_h_words": Wi_h_words,
        "Wi_h_scales": Wi_h_scales,
        "Wf_x_words": Wf_x_words,
        "Wf_x_scales": Wf_x_scales,
        "b_f": b_f,
        "Wf_h_words": Wf_h_words,
        "Wf_h_scales": Wf_h_scales,
    }


def reference(x, h_prev, m_prev, Wi_x_words, Wi_x_scales, b_i, Wi_h_words, Wi_h_scales, Wf_x_words, Wf_x_scales, b_f, Wf_h_words, Wf_h_scales):
    xq = mxq(f64(x), 1, "e5m2")
    hq = mxq(f64(h_prev), 1, "e5m2")
    i_tilde = (xq @ unpack4(Wi_x_words, Wi_x_scales)) + f64(b_i) + (hq @ unpack4(Wi_h_words, Wi_h_scales))
    f_aff = (xq @ unpack4(Wf_x_words, Wf_x_scales)) + f64(b_f) + (hq @ unpack4(Wf_h_words, Wf_h_scales))
    log_f = np.log(np.maximum(sigmoid(f_aff), 1e-8))
    m_t = np.maximum(log_f + f64(m_prev), i_tilde)
    i_prime = np.exp(i_tilde - m_t)
    f_prime = np.exp(log_f + f64(m_prev) - m_t)
    return m_t, i_prime, f_prime

@@ -1,0 +1,267 @@
+from contextlib import ExitStack
+
+import concourse.mybir as mybir
+from concourse.masks import make_identity
+
+B, IN, H = 512, 1024, 1024
+FLOPS = 2 * B * (IN + H) * 2 * H
+
+F32 = mybir.dt.float32
+BF16 = mybir.dt.bfloat16
+I32 = mybir.dt.int32
+U32 = mybir.dt.uint32
+U8 = mybir.dt.uint8
+E5M2X4 = mybir.dt.float8_e5m2_x4
+E2M1X4 = mybir.dt.float4_e2m1fn_x4
+ACT = mybir.ActivationFunctionType
+ALU = mybir.AluOpType
+
+P = 128
+PACK = 4
+K_PASS = P * PACK
+BANK = 512
+TOK_TILES = B // P
+CH_TILES = H // P
+HALVES = H // BANK
+GROUPS = IN // K_PASS
+PASSES = 2 * GROUPS
+BLOCKS = TOK_TILES * HALVES
+FLOOR = 1e-8
+
+
+def tile_slstmlayer_pa_kernel(
+    tc, x, h_prev, m_prev,
+    Wi_x_words, Wi_x_scales, b_i, Wi_h_words, Wi_h_scales,
+    Wf_x_words, Wf_x_scales, b_f, Wf_h_words, Wf_h_scales,
+    out_0, out_1, out_2,
+):
+    nc = tc.nc
+    with ExitStack() as ctx:
+        keep = ctx.enter_context(tc.tile_pool(name="keep", bufs=1))
+        psum = ctx.enter_context(tc.psum_pool(name="psum", bufs=1))
+        ctx.enter_context(tc.manual_schedule())
+
+        def sbuf(name, shape, dtype):
+            return keep.tile(shape, dtype, name=name, align_bytes=64)
+
+        def bank(number, name):
+            return psum.tile([P, BANK], F32, name=name, tag="bank%d" % number)
+
+        ident_f32 = sbuf("ident_f32", [P, P], F32)
+        ident_bf = sbuf("ident_bf", [P, P], BF16)
+        bias_rows = sbuf("bias_rows", [P, P], BF16)
+        nc.vector.memset(bias_rows[:], 0.0)
+        make_identity(nc, ident_f32[:])
+        make_identity(nc, ident_bf[:])
+        nc.scalar.dma_start(out=bias_rows[0:CH_TILES, :], in_=b_f.rearrange("(c n) -> c n", n=P))
+        nc.scalar.dma_start(out=bias_rows[CH_TILES : 2 * CH_TILES, :], in_=b_i.rearrange("(c n) -> c n", n=P))
+
+        planes = {}
+        for name in ("f_x", "f_h", "i_x", "i_h"):
+            planes[name] = sbuf("plane_" + name, [P, GROUPS, H], U8)
+            nc.vector.memset(planes[name][:].rearrange("p g n -> p (g n)").bitcast(I32), 0)
+
+        def load_scales(name, scales):
+            for q in range(4):
+                nc.sync.dma_start(
+                    out=planes[name][32 * q : 32 * q + 4, :, :].bitcast(I32),
+                    in_=scales[:, 4 * q : 4 * q + 4, :].rearrange("g r n -> r g n").bitcast(I32),
+                )
+
+        words = {}
+
+        def load_words(name, src, g):
+            words[name, g] = sbuf("words_%s%d" % (name, g), [P, 2 * H], U8)
+            nc.sync.dma_start(out=words[name, g][:].bitcast(I32), in_=src[g].bitcast(I32))
+
+        raw = []
+
+        def load_acts(src, g):
+            halves = []
+            for half in range(2):
+                tile = sbuf("raw%d_%d" % (len(raw), half), [P, 2, K_PASS], BF16)
+                rows = src[2 * P * half : 2 * P * (half + 1), g * K_PASS : (g + 1) * K_PASS]
+                nc.sync.dma_start(out=tile[:], in_=rows.rearrange("(t p) k -> p t k", p=P))
+                halves.append(tile)
+            raw.append(halves)
+
+        load_acts(x, 0)
+        load_acts(x, 1)
+        load_scales("f_x", Wf_x_scales)
+        load_scales("f_h", Wf_h_scales)
+        load_words("f_x", Wf_x_words, 0)
+        load_words("f_x", Wf_x_words, 1)
+        load_acts(h_prev, 0)
+        load_words("f_h", Wf_h_words, 0)
+        load_acts(h_prev, 1)
+        load_words("f_h", Wf_h_words, 1)
+        load_scales("i_x", Wi_x_scales)
+        load_scales("i_h", Wi_h_scales)
+        for g in range(GROUPS):
+            load_words("i_x", Wi_x_words, g)
+        for g in range(GROUPS):
+            load_words("i_h", Wi_h_words, g)
+        m_old = sbuf("m_old", [P, TOK_TILES, H], BF16)
+        nc.sync.dma_start(out=m_old[:], in_=m_prev.rearrange("(t p) n -> p t n", p=P))
+
+        sides = [(side, g) for side in ("x", "h") for g in range(GROUPS)]
+
+        codes = [sbuf("codes%d" % s, [P, B], U32) for s in range(PASSES)]
+        scales = [sbuf("scales%d" % s, [P, B], U8) for s in range(PASSES)]
+
+        def quantise_pass(s):
+            grouped = []
+            for half in range(2):
+                pairs = raw[s][half][:].rearrange("p t k -> p (t k)").bitcast(F32)
+                xt = bank(4 + 2 * (s % 2) + half, "xt%d_%d" % (s, half))
+                for tt in range(2):
+                    for u in range(2):
+                        nc.tensor.transpose(
+                            xt[:, (2 * tt + u) * P : (2 * tt + u + 1) * P],
+                            pairs[:, 256 * tt + u : 256 * (tt + 1) : 2],
+                            ident_f32[:],
+                        )
+                tile = sbuf("grouped%d_%d" % (s, half), [P, 2 * P * PACK], BF16)
+                dst = tile[:].bitcast(F32).rearrange("p (t r u) -> p t r u", t=2, u=2)
+                src = xt[:].rearrange("p (t u r) -> p t r u", t=2, u=2)
+                if half == 0:
+                    nc.scalar.copy(out=dst, in_=src)
+                else:
+                    nc.vector.tensor_copy(out=dst, in_=src)
+                grouped.append(tile)
+            for half in range(2):
+                cols = slice(256 * half, 256 * (half + 1))
+                nc.vector.quantize_mx(out=codes[s][:, cols].bitcast(E5M2X4), scales=scales[s][:, cols], in_=grouped[half][:])
+
+        f_ps = {}
+
+        def forget_pass(c, s):
+            side, g = sides[s]
+            if s == 0:
+                f_ps[c] = bank(c, "f_ps%d" % c)
+            nc.tensor.matmul_mx(
+                out=f_ps[c][:],
+                lhsT=words["f_" + side, g][:, 2 * P * c : 2 * P * (c + 1)].bitcast(E2M1X4),
+                lhsT_scale=planes["f_" + side][:, g, P * c : P * (c + 1)],
+                rhs=codes[s][:].bitcast(E5M2X4),
+                rhs_scale=scales[s][:],
+                start=(s == 0), stop=(s == PASSES - 1),
+            )
+
+        gate = {}
+
+        def forget_gate(c):
+            gate[c] = sbuf("gate%d" % c, [P, B], F32)
+            nc.scalar.activation(out=gate[c][:], in_=f_ps[c][:], func=ACT.Sigmoid, bias=bf_col[:, c : c + 1])
+            nc.vector.tensor_scalar(out=gate[c][:], in0=gate[c][:], scalar1=FLOOR, scalar2=None, op0=ALU.max)
+
+        quantise_pass(0)
+        quantise_pass(1)
+        bf_ps = bank(0, "bf_ps")
+        nc.tensor.matmul(bf_ps[:, 0:CH_TILES], lhsT=bias_rows[:], rhs=ident_bf[:, 0:CH_TILES], start=True, stop=True)
+        bf_col = sbuf("bf_col", [P, CH_TILES], F32)
+        nc.vector.tensor_copy(out=bf_col[:], in_=bf_ps[:, 0:CH_TILES])
+        bi_all = sbuf("bi_all", [P, H], F32)
+        for hf in range(HALVES):
+            bi_ps = bank(1 + hf, "bi_ps%d" % hf)
+            for c in range(4):
+                row = CH_TILES + 4 * hf + c
+                nc.tensor.matmul(
+                    bi_ps[:, c * P : (c + 1) * P],
+                    lhsT=ident_bf[:, row : row + 1].to_broadcast([P, P]),
+                    rhs=bias_rows[:], start=True, stop=True,
+                )
+            nc.scalar.copy(out=bi_all[:, hf * BANK : (hf + 1) * BANK], in_=bi_ps[:])
+
+        for s in range(PASSES):
+            for c in range(4):
+                forget_pass(c, s)
+            if s + 2 < PASSES:
+                quantise_pass(s + 2)
+        for c in range(4):
+            forget_gate(c)
+        for c in range(4, CH_TILES):
+            for s in range(PASSES):
+                forget_pass(c, s)
+            forget_gate(c)
+
+        log_f = {}
+        for c in range(CH_TILES):
+            log_f[c] = sbuf("log_f%d" % c, [P, B], F32)
+            nc.scalar.activation(out=log_f[c][:], in_=gate[c][:], func=ACT.Ln)
+
+        def where(j):
+            return j % TOK_TILES, j // TOK_TILES
+
+        i_ps, i_sb, a_ps, m_sb, di, df = {}, {}, {}, {}, {}, {}
+
+        def input_matmuls(j):
+            t, hf = where(j)
+            i_ps[j] = bank(j % 4, "i_ps%d" % j)
+            for s in range(PASSES):
+                side, g = sides[s]
+                nc.tensor.matmul_mx(
+                    out=i_ps[j][:],
+                    lhsT=codes[s][:, P * t : P * (t + 1)].bitcast(E5M2X4),
+                    lhsT_scale=scales[s][:, P * t : P * (t + 1)],
+                    rhs=words["i_" + side, g][:, 2 * BANK * hf : 2 * BANK * (hf + 1)].bitcast(E2M1X4),
+                    rhs_scale=planes["i_" + side][:, g, BANK * hf : BANK * (hf + 1)],
+                    start=(s == 0), stop=(s == PASSES - 1),
+                )
+
+        def add_input_bias(j):
+            hf = where(j)[1]
+            i_sb[j] = sbuf("i_sb%d" % j, [P, BANK], F32)
+            nc.vector.tensor_tensor(out=i_sb[j][:], in0=i_ps[j][:], in1=bi_all[:, BANK * hf : BANK * (hf + 1)], op=ALU.add)
+
+        def forget_sum(j):
+            t, hf = where(j)
+            a_ps[j] = bank(4 + j % 4, "a_ps%d" % j)
+            nc.tensor.matmul(a_ps[j][:], lhsT=ident_bf[:], rhs=m_old[:, t, BANK * hf : BANK * (hf + 1)], start=True, stop=False)
+            for c in range(4):
+                nc.tensor.matmul(
+                    a_ps[j][:, P * c : P * (c + 1)],
+                    lhsT=log_f[4 * hf + c][:, P * t : P * (t + 1)], rhs=ident_f32[:],
+                    is_transpose=True, start=False, stop=(c == 3),
+                )
+
+        def stabiliser(j):
+            m_sb[j] = sbuf("m_sb%d" % j, [P, BANK], F32)
+            nc.vector.tensor_tensor(out=m_sb[j][:], in0=a_ps[j][:], in1=i_sb[j][:], op=ALU.max)
+            di[j] = sbuf("di%d" % j, [P, BANK], F32)
+            nc.gpsimd.tensor_tensor(out=di[j][:], in0=i_sb[j][:], in1=m_sb[j][:], op=ALU.subtract)
+
+        def forget_diff(j):
+            df[j] = sbuf("df%d" % j, [P, BANK], F32)
+            nc.vector.tensor_tensor(out=df[j][:], in0=a_ps[j][:], in1=m_sb[j][:], op=ALU.subtract)
+
+        def store(out, j, tile):
+            t, hf = where(j)
+            nc.sync.dma_start(out=out[P * t : P * (t + 1), BANK * hf : BANK * (hf + 1)], in_=tile[:])
+
+        def exponentials(j):
+            nc.scalar.activation(out=df[j][:], in_=df[j][:], func=ACT.Exp)
+            nc.scalar.activation(out=di[j][:], in_=di[j][:], func=ACT.Exp)
+            if j >= 3 and j + 1 < BLOCKS:
+                store(out_0, j + 1, m_sb[j + 1])
+            store(out_2, j, df[j])
+            store(out_1, j, di[j])
+
+        for j in range(4):
+            input_matmuls(j)
+            add_input_bias(j)
+        for j in range(4):
+            forget_sum(j)
+            stabiliser(j)
+            store(out_0, j, m_sb[j])
+            if j > 0:
+                forget_diff(j - 1)
+        for j in range(4, BLOCKS):
+            input_matmuls(j)
+            add_input_bias(j)
+            forget_diff(j - 1)
+            forget_sum(j)
+            stabiliser(j)
+        forget_diff(BLOCKS - 1)
+        for j in range(BLOCKS):
+            exponentials(j)

@@ -50,11 +50,11 @@ def tile_slstmlayer_pa_kernel(
         ident_f32 = sbuf("ident_f32", [P, P], F32)
         ident_bf = sbuf("ident_bf", [P, P], BF16)
         bias_rows = sbuf("bias_rows", [P, P], BF16)
-        nc.vector.memset(bias_rows[:], 0.0)
         make_identity(nc, ident_f32[:])
+        nc.gpsimd.memset(bias_rows[:], 0.0)
+        nc.gpsimd.dma_start(out=bias_rows[0:CH_TILES, :], in_=b_f.rearrange("(c n) -> c n", n=P))
+        nc.gpsimd.dma_start(out=bias_rows[CH_TILES : 2 * CH_TILES, :], in_=b_i.rearrange("(c n) -> c n", n=P))
         make_identity(nc, ident_bf[:])
-        nc.scalar.dma_start(out=bias_rows[0:CH_TILES, :], in_=b_f.rearrange("(c n) -> c n", n=P))
-        nc.scalar.dma_start(out=bias_rows[CH_TILES : 2 * CH_TILES, :], in_=b_i.rearrange("(c n) -> c n", n=P))
 
         planes = {}
         for name in ("f_x", "f_h", "i_x", "i_h"):
@@ -62,10 +62,10 @@ def tile_slstmlayer_pa_kernel(
             nc.vector.memset(planes[name][:].rearrange("p g n -> p (g n)").bitcast(I32), 0)
 
         def load_scales(name, scales):
-            for q in range(4):
+            for r in range(4):
                 nc.sync.dma_start(
-                    out=planes[name][32 * q : 32 * q + 4, :, :].bitcast(I32),
-                    in_=scales[:, 4 * q : 4 * q + 4, :].rearrange("g r n -> r g n").bitcast(I32),
+                    out=planes[name][r:P:32, :, :].bitcast(I32),
+                    in_=scales[:, r:16:4, :].rearrange("g q n -> q g n").bitcast(I32),
                 )
 
         words = {}
@@ -76,24 +76,25 @@ def tile_slstmlayer_pa_kernel(
 
         raw = []
 
-        def load_acts(src, g):
+        def load_acts(src, g, pieces):
+            tiles = TOK_TILES // pieces
             halves = []
-            for half in range(2):
-                tile = sbuf("raw%d_%d" % (len(raw), half), [P, 2, K_PASS], BF16)
-                rows = src[2 * P * half : 2 * P * (half + 1), g * K_PASS : (g + 1) * K_PASS]
+            for piece in range(pieces):
+                tile = sbuf("raw%d_%d" % (len(raw), piece), [P, tiles, K_PASS], BF16)
+                rows = src[tiles * P * piece : tiles * P * (piece + 1), g * K_PASS : (g + 1) * K_PASS]
                 nc.sync.dma_start(out=tile[:], in_=rows.rearrange("(t p) k -> p t k", p=P))
-                halves.append(tile)
+                halves.extend(tile[:, first : first + 2, :] for first in range(0, tiles, 2))
             raw.append(halves)
 
-        load_acts(x, 0)
-        load_acts(x, 1)
+        load_acts(x, 0, 2)
+        load_acts(x, 1, 1)
         load_scales("f_x", Wf_x_scales)
-        load_scales("f_h", Wf_h_scales)
         load_words("f_x", Wf_x_words, 0)
         load_words("f_x", Wf_x_words, 1)
-        load_acts(h_prev, 0)
+        load_acts(h_prev, 0, 1)
+        load_acts(h_prev, 1, 1)
+        load_scales("f_h", Wf_h_scales)
         load_words("f_h", Wf_h_words, 0)
-        load_acts(h_prev, 1)
         load_words("f_h", Wf_h_words, 1)
         load_scales("i_x", Wi_x_scales)
         load_scales("i_h", Wi_h_scales)
@@ -109,29 +110,33 @@ def tile_slstmlayer_pa_kernel(
         codes = [sbuf("codes%d" % s, [P, B], U32) for s in range(PASSES)]
         scales = [sbuf("scales%d" % s, [P, B], U8) for s in range(PASSES)]
 
-        def quantise_pass(s):
-            grouped = []
+        split = {}
+
+        def split_words(s):
             for half in range(2):
-                pairs = raw[s][half][:].rearrange("p t k -> p (t k)").bitcast(F32)
-                xt = bank(4 + 2 * (s % 2) + half, "xt%d_%d" % (s, half))
+                pairs = raw[s][half].rearrange("p t k -> p (t k)").bitcast(F32)
+                split[s, half] = sbuf("split%d_%d" % (s, half), [P, 2, 2, P], F32)
+                nc.vector.tensor_copy(out=split[s, half][:], in_=pairs.rearrange("p (t w u) -> p t u w", t=2, u=2))
+
+        grouped = {}
+
+        def transpose_pass(s, first_bank):
+            for half in range(2):
+                xt = bank(first_bank + half, "xt%d_%d" % (s, half))
                 for tt in range(2):
                     for u in range(2):
-                        nc.tensor.transpose(
-                            xt[:, (2 * tt + u) * P : (2 * tt + u + 1) * P],
-                            pairs[:, 256 * tt + u : 256 * (tt + 1) : 2],
-                            ident_f32[:],
-                        )
-                tile = sbuf("grouped%d_%d" % (s, half), [P, 2 * P * PACK], BF16)
-                dst = tile[:].bitcast(F32).rearrange("p (t r u) -> p t r u", t=2, u=2)
-                src = xt[:].rearrange("p (t u r) -> p t r u", t=2, u=2)
-                if half == 0:
-                    nc.scalar.copy(out=dst, in_=src)
-                else:
-                    nc.vector.tensor_copy(out=dst, in_=src)
-                grouped.append(tile)
+                        nc.tensor.transpose(xt[:, (2 * tt + u) * P : (2 * tt + u + 1) * P], split[s, half][:, tt, u, :], ident_f32[:])
+                grouped[s, half] = sbuf("grouped%d_%d" % (s, half), [P, 2 * P * PACK], BF16)
+                copy = nc.vector.tensor_copy if s == PASSES - 1 else nc.scalar.copy
+                copy(
+                    out=grouped[s, half][:].bitcast(F32).rearrange("p (t r u) -> p t r u", t=2, u=2),
+                    in_=xt[:].rearrange("p (t u r) -> p t r u", t=2, u=2),
+                )
+
+        def quantise_pass(s):
             for half in range(2):
                 cols = slice(256 * half, 256 * (half + 1))
-                nc.vector.quantize_mx(out=codes[s][:, cols].bitcast(E5M2X4), scales=scales[s][:, cols], in_=grouped[half][:])
+                nc.vector.quantize_mx(out=codes[s][:, cols].bitcast(E5M2X4), scales=scales[s][:, cols], in_=grouped[s, half][:])
 
         f_ps = {}
 
@@ -155,33 +160,43 @@ def tile_slstmlayer_pa_kernel(
             nc.scalar.activation(out=gate[c][:], in_=f_ps[c][:], func=ACT.Sigmoid, bias=bf_col[:, c : c + 1])
             nc.vector.tensor_scalar(out=gate[c][:], in0=gate[c][:], scalar1=FLOOR, scalar2=None, op0=ALU.max)
 
+        split_words(0)
+        transpose_pass(0, 6)
+        split_words(1)
         quantise_pass(0)
+        transpose_pass(1, 4)
         quantise_pass(1)
-        bf_ps = bank(0, "bf_ps")
+        bf_ps = bank(6, "bf_ps")
         nc.tensor.matmul(bf_ps[:, 0:CH_TILES], lhsT=bias_rows[:], rhs=ident_bf[:, 0:CH_TILES], start=True, stop=True)
         bf_col = sbuf("bf_col", [P, CH_TILES], F32)
         nc.vector.tensor_copy(out=bf_col[:], in_=bf_ps[:, 0:CH_TILES])
-        bi_all = sbuf("bi_all", [P, H], F32)
-        for hf in range(HALVES):
-            bi_ps = bank(1 + hf, "bi_ps%d" % hf)
-            for c in range(4):
-                row = CH_TILES + 4 * hf + c
-                nc.tensor.matmul(
-                    bi_ps[:, c * P : (c + 1) * P],
-                    lhsT=ident_bf[:, row : row + 1].to_broadcast([P, P]),
-                    rhs=bias_rows[:], start=True, stop=True,
-                )
-            nc.scalar.copy(out=bi_all[:, hf * BANK : (hf + 1) * BANK], in_=bi_ps[:])
+        bi_ps = psum.tile([P, H], BF16, name="bi_ps", tag="bank7")
+        for c in range(CH_TILES):
+            row = CH_TILES + c
+            nc.tensor.matmul(
+                bi_ps[:, c * P : (c + 1) * P],
+                lhsT=ident_bf[:, row : row + 1].to_broadcast([P, P]),
+                rhs=bias_rows[:], start=True, stop=True,
+            )
+        bi_all = sbuf("bi_all", [P, H], BF16)
+        nc.scalar.copy(out=bi_all[:], in_=bi_ps[:])
 
-        for s in range(PASSES):
+        for s in range(GROUPS):
             for c in range(4):
                 forget_pass(c, s)
-            if s + 2 < PASSES:
-                quantise_pass(s + 2)
-        for c in range(4):
-            forget_gate(c)
-        for c in range(4, CH_TILES):
-            for s in range(PASSES):
+        split_words(2)
+        transpose_pass(2, 6)
+        split_words(3)
+        quantise_pass(2)
+        for s in range(GROUPS):
+            for c in (4, 5):
+                forget_pass(c, s)
+        transpose_pass(3, 6)
+        quantise_pass(3)
+        for c in range(6):
+            forget_pass(c, 2)
+        for c in range(CH_TILES):
+            for s in range(3 if c < 6 else 0, PASSES):
                 forget_pass(c, s)
             forget_gate(c)
 
@@ -214,10 +229,13 @@ def tile_slstmlayer_pa_kernel(
             i_sb[j] = sbuf("i_sb%d" % j, [P, BANK], F32)
             nc.vector.tensor_tensor(out=i_sb[j][:], in0=i_ps[j][:], in1=bi_all[:, BANK * hf : BANK * (hf + 1)], op=ALU.add)
 
-        def forget_sum(j):
+        def open_forget_sum(j):
             t, hf = where(j)
             a_ps[j] = bank(4 + j % 4, "a_ps%d" % j)
             nc.tensor.matmul(a_ps[j][:], lhsT=ident_bf[:], rhs=m_old[:, t, BANK * hf : BANK * (hf + 1)], start=True, stop=False)
+
+        def forget_sum(j):
+            t, hf = where(j)
             for c in range(4):
                 nc.tensor.matmul(
                     a_ps[j][:, P * c : P * (c + 1)],
@@ -251,6 +269,8 @@ def tile_slstmlayer_pa_kernel(
             input_matmuls(j)
             add_input_bias(j)
         for j in range(4):
+            open_forget_sum(j)
+        for j in range(4):
             forget_sum(j)
             stabiliser(j)
             store(out_0, j, m_sb[j])
@@ -260,6 +280,7 @@ def tile_slstmlayer_pa_kernel(
             input_matmuls(j)
             add_input_bias(j)
             forget_diff(j - 1)
+            open_forget_sum(j)
             forget_sum(j)
             stabiliser(j)
         forget_diff(BLOCKS - 1)

@@ -87,9 +87,9 @@ def tile_slstmlayer_pa_kernel(
             raw.append(halves)
 
         load_acts(x, 0, 2)
-        load_acts(x, 1, 1)
         load_scales("f_x", Wf_x_scales)
         load_words("f_x", Wf_x_words, 0)
+        load_acts(x, 1, 1)
         load_words("f_x", Wf_x_words, 1)
         load_acts(h_prev, 0, 1)
         load_acts(h_prev, 1, 1)
@@ -120,9 +120,9 @@ def tile_slstmlayer_pa_kernel(
 
         grouped = {}
 
-        def transpose_pass(s, first_bank):
+        def transpose_pass(s):
             for half in range(2):
-                xt = bank(first_bank + half, "xt%d_%d" % (s, half))
+                xt = bank(6 + half, "xt%d_%d" % (s, half))
                 for tt in range(2):
                     for u in range(2):
                         nc.tensor.transpose(xt[:, (2 * tt + u) * P : (2 * tt + u + 1) * P], split[s, half][:, tt, u, :], ident_f32[:])
@@ -153,24 +153,21 @@ def tile_slstmlayer_pa_kernel(
                 start=(s == 0), stop=(s == PASSES - 1),
             )
 
-        gate = {}
+        gate = [sbuf("gate%d" % pair, [P, 2, B], F32) for pair in range(CH_TILES // 2)]
 
         def forget_gate(c):
-            gate[c] = sbuf("gate%d" % c, [P, B], F32)
-            nc.scalar.activation(out=gate[c][:], in_=f_ps[c][:], func=ACT.Sigmoid, bias=bf_col[:, c : c + 1])
-            nc.vector.tensor_scalar(out=gate[c][:], in0=gate[c][:], scalar1=FLOOR, scalar2=None, op0=ALU.max)
+            dst = gate[c // 2][:, c % 2, :]
+            nc.scalar.activation(out=dst, in_=f_ps[c][:], func=ACT.Sigmoid, bias=bf_col[:, c : c + 1])
+            nc.vector.tensor_scalar(out=dst, in0=dst, scalar1=FLOOR, scalar2=None, op0=ALU.max)
 
         split_words(0)
-        transpose_pass(0, 6)
-        split_words(1)
+        transpose_pass(0)
         quantise_pass(0)
-        transpose_pass(1, 4)
-        quantise_pass(1)
-        bf_ps = bank(6, "bf_ps")
+        bf_ps = bank(4, "bf_ps")
         nc.tensor.matmul(bf_ps[:, 0:CH_TILES], lhsT=bias_rows[:], rhs=ident_bf[:, 0:CH_TILES], start=True, stop=True)
         bf_col = sbuf("bf_col", [P, CH_TILES], F32)
         nc.vector.tensor_copy(out=bf_col[:], in_=bf_ps[:, 0:CH_TILES])
-        bi_ps = psum.tile([P, H], BF16, name="bi_ps", tag="bank7")
+        bi_ps = psum.tile([P, H], BF16, name="bi_ps", tag="bank5")
         for c in range(CH_TILES):
             row = CH_TILES + c
             nc.tensor.matmul(
@@ -181,37 +178,45 @@ def tile_slstmlayer_pa_kernel(
         bi_all = sbuf("bi_all", [P, H], BF16)
         nc.scalar.copy(out=bi_all[:], in_=bi_ps[:])
 
-        for s in range(GROUPS):
-            for c in range(4):
+        def forget_passes(tiles, s):
+            for c in tiles:
                 forget_pass(c, s)
+
+        forget_passes(range(4), 0)
+        split_words(1)
+        transpose_pass(1)
+        forget_passes((4, 5), 0)
         split_words(2)
-        transpose_pass(2, 6)
+        quantise_pass(1)
+        transpose_pass(2)
+        forget_passes(range(3), 1)
         split_words(3)
         quantise_pass(2)
-        for s in range(GROUPS):
-            for c in (4, 5):
-                forget_pass(c, s)
-        transpose_pass(3, 6)
+        transpose_pass(3)
+        forget_passes(range(3, 6), 1)
         quantise_pass(3)
-        for c in range(6):
-            forget_pass(c, 2)
+        forget_passes(range(4), 2)
         for c in range(CH_TILES):
-            for s in range(3 if c < 6 else 0, PASSES):
+            for s in range(3 if c < 4 else 2 if c < 6 else 0, PASSES):
                 forget_pass(c, s)
             forget_gate(c)
 
         log_f = {}
-        for c in range(CH_TILES):
-            log_f[c] = sbuf("log_f%d" % c, [P, B], F32)
-            nc.scalar.activation(out=log_f[c][:], in_=gate[c][:], func=ACT.Ln)
+        for half in range(2):
+            for pair in range(CH_TILES // 2):
+                log_f[half, pair] = sbuf("log_f%d_%d" % (half, pair), [P, 2, 2 * P], F32)
+                nc.scalar.activation(out=log_f[half, pair][:], in_=gate[pair][:, :, 2 * P * half : 2 * P * (half + 1)], func=ACT.Ln)
 
-        def where(j):
-            return j % TOK_TILES, j // TOK_TILES
+        i_ps, i_sb, a_ps = {}, {}, {}
+        m_new = [sbuf("m_new%d" % t, [P, H], F32) for t in range(TOK_TILES)]
+        gap_i = [sbuf("gap_i%d" % t, [P, H], F32) for t in range(TOK_TILES)]
+        gap_f = [sbuf("gap_f%d" % t, [P, H], F32) for t in range(TOK_TILES)]
 
-        i_ps, i_sb, a_ps, m_sb, di, df = {}, {}, {}, {}, {}, {}
+        def cols(j):
+            return slice(BANK * (j % 2), BANK * (j % 2 + 1))
 
         def input_matmuls(j):
-            t, hf = where(j)
+            t, hf = divmod(j, 2)
             i_ps[j] = bank(j % 4, "i_ps%d" % j)
             for s in range(PASSES):
                 side, g = sides[s]
@@ -220,69 +225,77 @@ def tile_slstmlayer_pa_kernel(
                     lhsT=codes[s][:, P * t : P * (t + 1)].bitcast(E5M2X4),
                     lhsT_scale=scales[s][:, P * t : P * (t + 1)],
                     rhs=words["i_" + side, g][:, 2 * BANK * hf : 2 * BANK * (hf + 1)].bitcast(E2M1X4),
-                    rhs_scale=planes["i_" + side][:, g, BANK * hf : BANK * (hf + 1)],
+                    rhs_scale=planes["i_" + side][:, g, cols(j)],
                     start=(s == 0), stop=(s == PASSES - 1),
                 )
 
-        def add_input_bias(j):
-            hf = where(j)[1]
+        def input_bias(j):
             i_sb[j] = sbuf("i_sb%d" % j, [P, BANK], F32)
-            nc.vector.tensor_tensor(out=i_sb[j][:], in0=i_ps[j][:], in1=bi_all[:, BANK * hf : BANK * (hf + 1)], op=ALU.add)
+            nc.vector.tensor_tensor(out=i_sb[j][:], in0=bi_all[:, cols(j)], in1=i_ps[j][:], op=ALU.add)
 
-        def open_forget_sum(j):
-            t, hf = where(j)
+        def open_sum(j):
             a_ps[j] = bank(4 + j % 4, "a_ps%d" % j)
-            nc.tensor.matmul(a_ps[j][:], lhsT=ident_bf[:], rhs=m_old[:, t, BANK * hf : BANK * (hf + 1)], start=True, stop=False)
+            nc.tensor.matmul(a_ps[j][:], lhsT=ident_bf[:], rhs=m_old[:, j // 2, cols(j)], start=True, stop=False)
 
-        def forget_sum(j):
-            t, hf = where(j)
+        def close_sum(j):
+            t = j // 2
             for c in range(4):
-                nc.tensor.matmul(
-                    a_ps[j][:, P * c : P * (c + 1)],
-                    lhsT=log_f[4 * hf + c][:, P * t : P * (t + 1)], rhs=ident_f32[:],
-                    is_transpose=True, start=False, stop=(c == 3),
-                )
+                src = log_f[t // 2, 2 * (j % 2) + c // 2][:, c % 2, P * (t % 2) : P * (t % 2 + 1)]
+                nc.tensor.matmul(a_ps[j][:, P * c : P * (c + 1)], lhsT=src, rhs=ident_f32[:], is_transpose=True, start=False, stop=(c == 3))
+
+        def store(out, t, tile, span):
+            nc.sync.dma_start(out=out[P * t : P * (t + 1), span], in_=tile[t][:, span])
 
         def stabiliser(j):
-            m_sb[j] = sbuf("m_sb%d" % j, [P, BANK], F32)
-            nc.vector.tensor_tensor(out=m_sb[j][:], in0=a_ps[j][:], in1=i_sb[j][:], op=ALU.max)
-            di[j] = sbuf("di%d" % j, [P, BANK], F32)
-            nc.gpsimd.tensor_tensor(out=di[j][:], in0=i_sb[j][:], in1=m_sb[j][:], op=ALU.subtract)
+            t = j // 2
+            nc.vector.tensor_tensor(out=m_new[t][:, cols(j)], in0=i_sb[j][:], in1=a_ps[j][:], op=ALU.max)
+            nc.gpsimd.tensor_tensor(out=gap_i[t][:, cols(j)], in0=m_new[t][:, cols(j)], in1=i_sb[j][:], op=ALU.subtract)
 
-        def forget_diff(j):
-            df[j] = sbuf("df%d" % j, [P, BANK], F32)
-            nc.vector.tensor_tensor(out=df[j][:], in0=a_ps[j][:], in1=m_sb[j][:], op=ALU.subtract)
+        def forget_gap(j):
+            t = j // 2
+            nc.vector.tensor_tensor(out=gap_f[t][:, cols(j)], in0=m_new[t][:, cols(j)], in1=a_ps[j][:], op=ALU.subtract)
 
-        def store(out, j, tile):
-            t, hf = where(j)
-            nc.sync.dma_start(out=out[P * t : P * (t + 1), BANK * hf : BANK * (hf + 1)], in_=tile[:])
+        def exponential(out, t, gap, span):
+            nc.scalar.activation(out=gap[t][:, span], in_=gap[t][:, span], func=ACT.Exp, scale=-1.0)
+            store(out, t, gap, span)
 
-        def exponentials(j):
-            nc.scalar.activation(out=df[j][:], in_=df[j][:], func=ACT.Exp)
-            nc.scalar.activation(out=di[j][:], in_=di[j][:], func=ACT.Exp)
-            if j >= 3 and j + 1 < BLOCKS:
-                store(out_0, j + 1, m_sb[j + 1])
-            store(out_2, j, df[j])
-            store(out_1, j, di[j])
+        whole = slice(0, H)
 
-        for j in range(4):
+        for j in range(3):
             input_matmuls(j)
-            add_input_bias(j)
+            input_bias(j)
         for j in range(4):
-            open_forget_sum(j)
-        for j in range(4):
-            forget_sum(j)
+            open_sum(j)
+        for j in range(3):
+            close_sum(j)
             stabiliser(j)
-            store(out_0, j, m_sb[j])
-            if j > 0:
-                forget_diff(j - 1)
-        for j in range(4, BLOCKS):
-            input_matmuls(j)
-            add_input_bias(j)
-            forget_diff(j - 1)
-            open_forget_sum(j)
-            forget_sum(j)
-            stabiliser(j)
-        forget_diff(BLOCKS - 1)
-        for j in range(BLOCKS):
-            exponentials(j)
+        store(out_0, 0, m_new, whole)
+        store(out_0, 1, m_new, cols(2))
+        input_matmuls(3)
+        input_bias(3)
+        close_sum(3)
+        forget_gap(0)
+        stabiliser(3)
+        store(out_0, 1, m_new, cols(3))
+        for j in range(1, 4):
+            forget_gap(j)
+        for j in range(2):
+            exponential(out_2, 0, gap_f, cols(j))
+            exponential(out_1, 0, gap_i, cols(j))
+        for t in (2, 3):
+            blocks = (2 * t, 2 * t + 1)
+            for j in blocks:
+                input_matmuls(j)
+                input_bias(j)
+            for j in blocks:
+                open_sum(j)
+            for j in blocks:
+                close_sum(j)
+                stabiliser(j)
+            exponential(out_2, t - 1, gap_f, whole)
+            store(out_0, t, m_new, whole)
+            exponential(out_1, t - 1, gap_i, whole)
+            for j in blocks:
+                forget_gap(j)
+        exponential(out_2, 3, gap_f, whole)
+        exponential(out_1, 3, gap_i, whole)

@@ -51,9 +51,9 @@ def tile_slstmlayer_pa_kernel(
         ident_bf = sbuf("ident_bf", [P, P], BF16)
         bias_rows = sbuf("bias_rows", [P, P], BF16)
         make_identity(nc, ident_f32[:])
-        nc.gpsimd.memset(bias_rows[:], 0.0)
-        nc.gpsimd.dma_start(out=bias_rows[0:CH_TILES, :], in_=b_f.rearrange("(c n) -> c n", n=P))
-        nc.gpsimd.dma_start(out=bias_rows[CH_TILES : 2 * CH_TILES, :], in_=b_i.rearrange("(c n) -> c n", n=P))
+        nc.vector.memset(bias_rows[:], 0.0)
+        nc.scalar.dma_start(out=bias_rows[0:CH_TILES, :], in_=b_f.rearrange("(c n) -> c n", n=P))
+        nc.scalar.dma_start(out=bias_rows[CH_TILES : 2 * CH_TILES, :], in_=b_i.rearrange("(c n) -> c n", n=P))
         make_identity(nc, ident_bf[:])
 
         planes = {}

@@ -27,6 +27,7 @@ GROUPS = IN // K_PASS
 PASSES = 2 * GROUPS
 BLOCKS = TOK_TILES * HALVES
 FLOOR = 1e-8
+WARM_UPS = 5
 
 
 def tile_slstmlayer_pa_kernel(
@@ -50,6 +51,11 @@ def tile_slstmlayer_pa_kernel(
         ident_f32 = sbuf("ident_f32", [P, P], F32)
         ident_bf = sbuf("ident_bf", [P, P], BF16)
         bias_rows = sbuf("bias_rows", [P, P], BF16)
+        warm = sbuf("warm", [P, BANK], BF16)
+        nc.vector.memset(warm[:].bitcast(I32), 0)
+        warm_ps = bank(0, "warm_ps")
+        for step in range(WARM_UPS):
+            nc.tensor.matmul(warm_ps[:], lhsT=warm[:, 0:P], rhs=warm[:], start=True, stop=True)
         make_identity(nc, ident_f32[:])
         nc.vector.memset(bias_rows[:], 0.0)
         nc.scalar.dma_start(out=bias_rows[0:CH_TILES, :], in_=b_f.rearrange("(c n) -> c n", n=P))

from contextlib import ExitStack

import concourse.mybir as mybir
from concourse.masks import make_identity

B, IN, H = 512, 1024, 1024
FLOPS = 2 * B * (IN + H) * 2 * H

F32 = mybir.dt.float32
BF16 = mybir.dt.bfloat16
I32 = mybir.dt.int32
U32 = mybir.dt.uint32
U8 = mybir.dt.uint8
E5M2X4 = mybir.dt.float8_e5m2_x4
E2M1X4 = mybir.dt.float4_e2m1fn_x4
ACT = mybir.ActivationFunctionType
ALU = mybir.AluOpType

P = 128
PACK = 4
K_PASS = P * PACK
BANK = 512
TOK_TILES = B // P
CH_TILES = H // P
HALVES = H // BANK
GROUPS = IN // K_PASS
PASSES = 2 * GROUPS
BLOCKS = TOK_TILES * HALVES
FLOOR = 1e-8
WARM_UPS = 5


def tile_slstmlayer_pa_kernel(
    tc, x, h_prev, m_prev,
    Wi_x_words, Wi_x_scales, b_i, Wi_h_words, Wi_h_scales,
    Wf_x_words, Wf_x_scales, b_f, Wf_h_words, Wf_h_scales,
    out_0, out_1, out_2,
):
    nc = tc.nc
    with ExitStack() as ctx:
        keep = ctx.enter_context(tc.tile_pool(name="keep", bufs=1))
        psum = ctx.enter_context(tc.psum_pool(name="psum", bufs=1))
        ctx.enter_context(tc.manual_schedule())

        def sbuf(name, shape, dtype):
            return keep.tile(shape, dtype, name=name, align_bytes=64)

        def bank(number, name):
            return psum.tile([P, BANK], F32, name=name, tag="bank%d" % number)

        ident_f32 = sbuf("ident_f32", [P, P], F32)
        ident_bf = sbuf("ident_bf", [P, P], BF16)
        bias_rows = sbuf("bias_rows", [P, P], BF16)
        warm = sbuf("warm", [P, BANK], BF16)
        nc.vector.memset(warm[:].bitcast(I32), 0)
        warm_ps = bank(0, "warm_ps")
        for step in range(WARM_UPS):
            nc.tensor.matmul(warm_ps[:], lhsT=warm[:, 0:P], rhs=warm[:], start=True, stop=True)
        make_identity(nc, ident_f32[:])
        nc.vector.memset(bias_rows[:], 0.0)
        nc.scalar.dma_start(out=bias_rows[0:CH_TILES, :], in_=b_f.rearrange("(c n) -> c n", n=P))
        nc.scalar.dma_start(out=bias_rows[CH_TILES : 2 * CH_TILES, :], in_=b_i.rearrange("(c n) -> c n", n=P))
        make_identity(nc, ident_bf[:])

        planes = {}
        for name in ("f_x", "f_h", "i_x", "i_h"):
            planes[name] = sbuf("plane_" + name, [P, GROUPS, H], U8)
            nc.vector.memset(planes[name][:].rearrange("p g n -> p (g n)").bitcast(I32), 0)

        def load_scales(name, scales):
            for r in range(4):
                nc.sync.dma_start(
                    out=planes[name][r:P:32, :, :].bitcast(I32),
                    in_=scales[:, r:16:4, :].rearrange("g q n -> q g n").bitcast(I32),
                )

        words = {}

        def load_words(name, src, g):
            words[name, g] = sbuf("words_%s%d" % (name, g), [P, 2 * H], U8)
            nc.sync.dma_start(out=words[name, g][:].bitcast(I32), in_=src[g].bitcast(I32))

        raw = []

        def load_acts(src, g, pieces):
            tiles = TOK_TILES // pieces
            halves = []
            for piece in range(pieces):
                tile = sbuf("raw%d_%d" % (len(raw), piece), [P, tiles, K_PASS], BF16)
                rows = src[tiles * P * piece : tiles * P * (piece + 1), g * K_PASS : (g + 1) * K_PASS]
                nc.sync.dma_start(out=tile[:], in_=rows.rearrange("(t p) k -> p t k", p=P))
                halves.extend(tile[:, first : first + 2, :] for first in range(0, tiles, 2))
            raw.append(halves)

        load_acts(x, 0, 2)
        load_scales("f_x", Wf_x_scales)
        load_words("f_x", Wf_x_words, 0)
        load_acts(x, 1, 1)
        load_words("f_x", Wf_x_words, 1)
        load_acts(h_prev, 0, 1)
        load_acts(h_prev, 1, 1)
        load_scales("f_h", Wf_h_scales)
        load_words("f_h", Wf_h_words, 0)
        load_words("f_h", Wf_h_words, 1)
        load_scales("i_x", Wi_x_scales)
        load_scales("i_h", Wi_h_scales)
        for g in range(GROUPS):
            load_words("i_x", Wi_x_words, g)
        for g in range(GROUPS):
            load_words("i_h", Wi_h_words, g)
        m_old = sbuf("m_old", [P, TOK_TILES, H], BF16)
        nc.sync.dma_start(out=m_old[:], in_=m_prev.rearrange("(t p) n -> p t n", p=P))

        sides = [(side, g) for side in ("x", "h") for g in range(GROUPS)]

        codes = [sbuf("codes%d" % s, [P, B], U32) for s in range(PASSES)]
        scales = [sbuf("scales%d" % s, [P, B], U8) for s in range(PASSES)]

        split = {}

        def split_words(s):
            for half in range(2):
                pairs = raw[s][half].rearrange("p t k -> p (t k)").bitcast(F32)
                split[s, half] = sbuf("split%d_%d" % (s, half), [P, 2, 2, P], F32)
                nc.vector.tensor_copy(out=split[s, half][:], in_=pairs.rearrange("p (t w u) -> p t u w", t=2, u=2))

        grouped = {}

        def transpose_pass(s):
            for half in range(2):
                xt = bank(6 + half, "xt%d_%d" % (s, half))
                for tt in range(2):
                    for u in range(2):
                        nc.tensor.transpose(xt[:, (2 * tt + u) * P : (2 * tt + u + 1) * P], split[s, half][:, tt, u, :], ident_f32[:])
                grouped[s, half] = sbuf("grouped%d_%d" % (s, half), [P, 2 * P * PACK], BF16)
                copy = nc.vector.tensor_copy if s == PASSES - 1 else nc.scalar.copy
                copy(
                    out=grouped[s, half][:].bitcast(F32).rearrange("p (t r u) -> p t r u", t=2, u=2),
                    in_=xt[:].rearrange("p (t u r) -> p t r u", t=2, u=2),
                )

        def quantise_pass(s):
            for half in range(2):
                cols = slice(256 * half, 256 * (half + 1))
                nc.vector.quantize_mx(out=codes[s][:, cols].bitcast(E5M2X4), scales=scales[s][:, cols], in_=grouped[s, half][:])

        f_ps = {}

        def forget_pass(c, s):
            side, g = sides[s]
            if s == 0:
                f_ps[c] = bank(c, "f_ps%d" % c)
            nc.tensor.matmul_mx(
                out=f_ps[c][:],
                lhsT=words["f_" + side, g][:, 2 * P * c : 2 * P * (c + 1)].bitcast(E2M1X4),
                lhsT_scale=planes["f_" + side][:, g, P * c : P * (c + 1)],
                rhs=codes[s][:].bitcast(E5M2X4),
                rhs_scale=scales[s][:],
                start=(s == 0), stop=(s == PASSES - 1),
            )

        gate = [sbuf("gate%d" % pair, [P, 2, B], F32) for pair in range(CH_TILES // 2)]

        def forget_gate(c):
            dst = gate[c // 2][:, c % 2, :]
            nc.scalar.activation(out=dst, in_=f_ps[c][:], func=ACT.Sigmoid, bias=bf_col[:, c : c + 1])
            nc.vector.tensor_scalar(out=dst, in0=dst, scalar1=FLOOR, scalar2=None, op0=ALU.max)

        split_words(0)
        transpose_pass(0)
        quantise_pass(0)
        bf_ps = bank(4, "bf_ps")
        nc.tensor.matmul(bf_ps[:, 0:CH_TILES], lhsT=bias_rows[:], rhs=ident_bf[:, 0:CH_TILES], start=True, stop=True)
        bf_col = sbuf("bf_col", [P, CH_TILES], F32)
        nc.vector.tensor_copy(out=bf_col[:], in_=bf_ps[:, 0:CH_TILES])
        bi_ps = psum.tile([P, H], BF16, name="bi_ps", tag="bank5")
        for c in range(CH_TILES):
            row = CH_TILES + c
            nc.tensor.matmul(
                bi_ps[:, c * P : (c + 1) * P],
                lhsT=ident_bf[:, row : row + 1].to_broadcast([P, P]),
                rhs=bias_rows[:], start=True, stop=True,
            )
        bi_all = sbuf("bi_all", [P, H], BF16)
        nc.scalar.copy(out=bi_all[:], in_=bi_ps[:])

        def forget_passes(tiles, s):
            for c in tiles:
                forget_pass(c, s)

        forget_passes(range(4), 0)
        split_words(1)
        transpose_pass(1)
        forget_passes((4, 5), 0)
        split_words(2)
        quantise_pass(1)
        transpose_pass(2)
        forget_passes(range(3), 1)
        split_words(3)
        quantise_pass(2)
        transpose_pass(3)
        forget_passes(range(3, 6), 1)
        quantise_pass(3)
        forget_passes(range(4), 2)
        for c in range(CH_TILES):
            for s in range(3 if c < 4 else 2 if c < 6 else 0, PASSES):
                forget_pass(c, s)
            forget_gate(c)

        log_f = {}
        for half in range(2):
            for pair in range(CH_TILES // 2):
                log_f[half, pair] = sbuf("log_f%d_%d" % (half, pair), [P, 2, 2 * P], F32)
                nc.scalar.activation(out=log_f[half, pair][:], in_=gate[pair][:, :, 2 * P * half : 2 * P * (half + 1)], func=ACT.Ln)

        i_ps, i_sb, a_ps = {}, {}, {}
        m_new = [sbuf("m_new%d" % t, [P, H], F32) for t in range(TOK_TILES)]
        gap_i = [sbuf("gap_i%d" % t, [P, H], F32) for t in range(TOK_TILES)]
        gap_f = [sbuf("gap_f%d" % t, [P, H], F32) for t in range(TOK_TILES)]

        def cols(j):
            return slice(BANK * (j % 2), BANK * (j % 2 + 1))

        def input_matmuls(j):
            t, hf = divmod(j, 2)
            i_ps[j] = bank(j % 4, "i_ps%d" % j)
            for s in range(PASSES):
                side, g = sides[s]
                nc.tensor.matmul_mx(
                    out=i_ps[j][:],
                    lhsT=codes[s][:, P * t : P * (t + 1)].bitcast(E5M2X4),
                    lhsT_scale=scales[s][:, P * t : P * (t + 1)],
                    rhs=words["i_" + side, g][:, 2 * BANK * hf : 2 * BANK * (hf + 1)].bitcast(E2M1X4),
                    rhs_scale=planes["i_" + side][:, g, cols(j)],
                    start=(s == 0), stop=(s == PASSES - 1),
                )

        def input_bias(j):
            i_sb[j] = sbuf("i_sb%d" % j, [P, BANK], F32)
            nc.vector.tensor_tensor(out=i_sb[j][:], in0=bi_all[:, cols(j)], in1=i_ps[j][:], op=ALU.add)

        def open_sum(j):
            a_ps[j] = bank(4 + j % 4, "a_ps%d" % j)
            nc.tensor.matmul(a_ps[j][:], lhsT=ident_bf[:], rhs=m_old[:, j // 2, cols(j)], start=True, stop=False)

        def close_sum(j):
            t = j // 2
            for c in range(4):
                src = log_f[t // 2, 2 * (j % 2) + c // 2][:, c % 2, P * (t % 2) : P * (t % 2 + 1)]
                nc.tensor.matmul(a_ps[j][:, P * c : P * (c + 1)], lhsT=src, rhs=ident_f32[:], is_transpose=True, start=False, stop=(c == 3))

        def store(out, t, tile, span):
            nc.sync.dma_start(out=out[P * t : P * (t + 1), span], in_=tile[t][:, span])

        def stabiliser(j):
            t = j // 2
            nc.vector.tensor_tensor(out=m_new[t][:, cols(j)], in0=i_sb[j][:], in1=a_ps[j][:], op=ALU.max)
            nc.gpsimd.tensor_tensor(out=gap_i[t][:, cols(j)], in0=m_new[t][:, cols(j)], in1=i_sb[j][:], op=ALU.subtract)

        def forget_gap(j):
            t = j // 2
            nc.vector.tensor_tensor(out=gap_f[t][:, cols(j)], in0=m_new[t][:, cols(j)], in1=a_ps[j][:], op=ALU.subtract)

        def exponential(out, t, gap, span):
            nc.scalar.activation(out=gap[t][:, span], in_=gap[t][:, span], func=ACT.Exp, scale=-1.0)
            store(out, t, gap, span)

        whole = slice(0, H)

        for j in range(3):
            input_matmuls(j)
            input_bias(j)
        for j in range(4):
            open_sum(j)
        for j in range(3):
            close_sum(j)
            stabiliser(j)
        store(out_0, 0, m_new, whole)
        store(out_0, 1, m_new, cols(2))
        input_matmuls(3)
        input_bias(3)
        close_sum(3)
        forget_gap(0)
        stabiliser(3)
        store(out_0, 1, m_new, cols(3))
        for j in range(1, 4):
            forget_gap(j)
        for j in range(2):
            exponential(out_2, 0, gap_f, cols(j))
            exponential(out_1, 0, gap_i, cols(j))
        for t in (2, 3):
            blocks = (2 * t, 2 * t + 1)
            for j in blocks:
                input_matmuls(j)
                input_bias(j)
            for j in blocks:
                open_sum(j)
            for j in blocks:
                close_sum(j)
                stabiliser(j)
            exponential(out_2, t - 1, gap_f, whole)
            store(out_0, t, m_new, whole)
            exponential(out_1, t - 1, gap_i, whole)
            for j in blocks:
                forget_gap(j)
        exponential(out_2, 3, gap_f, whole)
        exponential(out_1, 3, gap_i, whole)
